import numpy as np
import ml_dtypes

BF16 = ml_dtypes.bfloat16


def bf(x):
    return np.asarray(x, np.float32).astype(BF16)


def f32(x):
    return np.asarray(x, np.float32)


def f64(x):
    return np.asarray(x).astype(np.float64)


def striped(idx):
    return np.tile(idx.reshape(-1, 16).T, (8, 1))


C, S, N, Q = 256, 4096, 2048, 128
STEP = 0.25
COEFF = -0.5 / STEP**2
AMP = np.sqrt(0.1 * Q * STEP / np.sqrt(C))


def silu(v):
    return v / (1.0 + np.exp(-v))


def setup_inputs():
    return {
        "x": f32(AMP * np.random.standard_normal((C, S))),
        "other": f32(AMP * np.random.standard_normal((C, N))),
        "centers": f32((np.arange(Q) - (Q - 1) / 2.0)[:, None] * STEP),
        "w1": bf(0.5 * np.random.standard_normal((Q, Q))),
        "b1": f32(0.1 * np.random.standard_normal((Q, 1))),
        "w2": bf(2.0 * np.random.standard_normal((Q, Q)) / np.sqrt(Q)),
        "b2": f32(0.1 * np.random.standard_normal((Q, 1))),
        "offs": striped(np.random.permutation(np.tile(np.arange(S), 2))[:N]),
    }


def reference(x, other, centers, w1, b1, w2, b2, offs):
    idx = offs[:16].T.reshape(-1)
    spin = np.sum(f64(x)[:, idx] * f64(other), axis=0, keepdims=True)
    gau = np.exp(COEFF * (spin - f64(centers)) ** 2)
    h = silu(f64(w1).T @ gau + f64(b1))
    return gau + silu(f64(w2).T @ h + f64(b2))

@@ -1,0 +1,84 @@
+import concourse.mybir as mybir
+
+F32 = mybir.dt.float32
+BF16 = mybir.dt.bfloat16
+U16 = mybir.dt.uint16
+FUNC = mybir.ActivationFunctionType
+MULT = mybir.AluOpType.mult
+ADD = mybir.AluOpType.add
+
+P = 128
+C, S, N, Q = 256, 4096, 2048, 128
+BLOCKS = C // P
+PIECE = 512
+PIECES = N // PIECE
+OFFSET_COLS = PIECE // 16
+
+FLOPS = 2 * C * N + 2 * (2 * Q * Q * N)
+
+
+def tile_spindistanceedge_kernel(tc, x, other, centers, w1, b1, w2, b2, offs, out):
+    nc = tc.nc
+    with (
+        tc.tile_pool(name="held", bufs=1) as held,
+        tc.psum_pool(name="banks", bufs=8) as banks,
+    ):
+        offsets = held.tile([P, N // 16], U16, name="offsets")
+        nc.sync.dma_start(offsets[:], offs)
+        table = []
+        target = []
+        for b in range(BLOCKS):
+            rows = slice(b * P, (b + 1) * P)
+            table.append(held.tile([P, S], F32, name=f"table{b}"))
+            nc.sync.dma_start(table[b][:], x[rows, :])
+            target.append([])
+            for k in range(PIECES):
+                target[b].append(held.tile([P, PIECE], F32, name=f"target{b}_{k}"))
+                nc.sync.dma_start(target[b][k][:], other[rows, k * PIECE : (k + 1) * PIECE])
+
+        w1_sb = held.tile([Q, Q], BF16, name="w1_sb")
+        w2_sb = held.tile([Q, Q], BF16, name="w2_sb")
+        centers_sb = held.tile([Q, 1], F32, name="centers_sb")
+        b1_sb = held.tile([Q, 1], F32, name="b1_sb")
+        b2_sb = held.tile([Q, 1], F32, name="b2_sb")
+        for tile, source in ((centers_sb, centers), (w1_sb, w1), (b1_sb, b1), (w2_sb, w2), (b2_sb, b2)):
+            nc.scalar.dma_start(tile[:], source)
+
+        ones = held.tile([P, Q], F32, name="ones")
+        nc.gpsimd.memset(ones[:], 1.0)
+        minus_centers = held.tile([Q, 1], F32, name="minus_centers")
+        nc.gpsimd.tensor_scalar_mul(minus_centers[:], centers_sb[:], -1.0)
+
+        spin = [banks.tile([Q, PIECE], F32, name=f"spin{k}", tag="bank") for k in range(PIECES)]
+        gau = [held.tile([Q, PIECE], F32, name=f"gau{k}") for k in range(PIECES)]
+        gau_bf = [held.tile([Q, PIECE], BF16, name=f"gau_bf{k}") for k in range(PIECES)]
+        for b in range(BLOCKS):
+            for k in range(PIECES):
+                product = held.tile([P, PIECE], F32, name=f"product{b}_{k}")
+                nc.vector.tensor_tensor(
+                    product[:],
+                    table[b][:].indirect(offsets[:, k * OFFSET_COLS : (k + 1) * OFFSET_COLS]),
+                    target[b][k][:],
+                    MULT,
+                )
+                nc.tensor.matmul(spin[k][:], ones[:], product[:], start=(b == 0), stop=(b == BLOCKS - 1))
+                if b == BLOCKS - 1:
+                    squared = held.tile([Q, PIECE], F32, name=f"squared{k}")
+                    nc.scalar.activation(squared[:], spin[k][:], FUNC.Square, bias=minus_centers[:])
+                    nc.scalar.activation(gau[k][:], squared[:], FUNC.Exp, scale=-8.0)
+                    nc.gpsimd.tensor_copy(gau_bf[k][:], gau[k][:])
+
+        hidden = []
+        for k in range(PIECES):
+            z1 = banks.tile([Q, PIECE], F32, name=f"z1_{k}", tag="bank")
+            nc.tensor.matmul(z1[:], w1_sb[:], gau_bf[k][:], start=True, stop=True)
+            hidden.append(held.tile([Q, PIECE], BF16, name=f"hidden{k}"))
+            nc.scalar.activation(hidden[k][:], z1[:], FUNC.Silu, bias=b1_sb[:])
+        for k in range(PIECES):
+            z2 = banks.tile([Q, PIECE], F32, name=f"z2_{k}", tag="bank")
+            nc.tensor.matmul(z2[:], w2_sb[:], hidden[k][:], start=True, stop=True)
+            layer = held.tile([Q, PIECE], F32, name=f"layer{k}")
+            nc.scalar.activation(layer[:], z2[:], FUNC.Silu, bias=b2_sb[:])
+            result = held.tile([Q, PIECE], F32, name=f"result{k}")
+            nc.vector.tensor_tensor(result[:], layer[:], gau[k][:], ADD)
+            nc.sync.dma_start(out[:, k * PIECE : (k + 1) * PIECE], result[:])

@@ -47,7 +47,7 @@ def tile_spindistanceedge_kernel(tc, x, other, centers, w1, b1, w2, b2, offs, ou
         ones = held.tile([P, Q], F32, name="ones")
         nc.gpsimd.memset(ones[:], 1.0)
         minus_centers = held.tile([Q, 1], F32, name="minus_centers")
-        nc.gpsimd.tensor_scalar_mul(minus_centers[:], centers_sb[:], -1.0)
+        nc.scalar.mul(minus_centers[:], centers_sb[:], -1.0)
 
         spin = [banks.tile([Q, PIECE], F32, name=f"spin{k}", tag="bank") for k in range(PIECES)]
         gau = [held.tile([Q, PIECE], F32, name=f"gau{k}") for k in range(PIECES)]

@@ -10,9 +10,11 @@ ADD = mybir.AluOpType.add
 P = 128
 C, S, N, Q = 256, 4096, 2048, 128
 BLOCKS = C // P
-PIECE = 512
-PIECES = N // PIECE
-OFFSET_COLS = PIECE // 16
+BANK = 512
+WIDTHS = (512, 512, 512, 256, 256)
+assert sum(WIDTHS) == N and max(WIDTHS) <= BANK
+STARTS = [sum(WIDTHS[:k]) for k in range(len(WIDTHS))]
+PIECES = [slice(start, start + width) for start, width in zip(STARTS, WIDTHS)]
 
 FLOPS = 2 * C * N + 2 * (2 * Q * Q * N)
 
@@ -21,6 +23,7 @@ def tile_spindistanceedge_kernel(tc, x, other, centers, w1, b1, w2, b2, offs, ou
     nc = tc.nc
     with (
         tc.tile_pool(name="held", bufs=1) as held,
+        tc.tile_pool(name="shared", bufs=1) as shared,
         tc.psum_pool(name="banks", bufs=8) as banks,
     ):
         offsets = held.tile([P, N // 16], U16, name="offsets")
@@ -31,10 +34,9 @@ def tile_spindistanceedge_kernel(tc, x, other, centers, w1, b1, w2, b2, offs, ou
             rows = slice(b * P, (b + 1) * P)
             table.append(held.tile([P, S], F32, name=f"table{b}"))
             nc.sync.dma_start(table[b][:], x[rows, :])
-            target.append([])
-            for k in range(PIECES):
-                target[b].append(held.tile([P, PIECE], F32, name=f"target{b}_{k}"))
-                nc.sync.dma_start(target[b][k][:], other[rows, k * PIECE : (k + 1) * PIECE])
+            target.append(held.tile([P, N], F32, name=f"target{b}"))
+            for start in range(0, N, BANK):
+                nc.sync.dma_start(target[b][:, start : start + BANK], other[rows, start : start + BANK])
 
         w1_sb = held.tile([Q, Q], BF16, name="w1_sb")
         w2_sb = held.tile([Q, Q], BF16, name="w2_sb")
@@ -49,36 +51,43 @@ def tile_spindistanceedge_kernel(tc, x, other, centers, w1, b1, w2, b2, offs, ou
         minus_centers = held.tile([Q, 1], F32, name="minus_centers")
         nc.scalar.mul(minus_centers[:], centers_sb[:], -1.0)
 
-        spin = [banks.tile([Q, PIECE], F32, name=f"spin{k}", tag="bank") for k in range(PIECES)]
-        gau = [held.tile([Q, PIECE], F32, name=f"gau{k}") for k in range(PIECES)]
-        gau_bf = [held.tile([Q, PIECE], BF16, name=f"gau_bf{k}") for k in range(PIECES)]
+        product = [held.tile([P, N], F32, name=f"product{b}") for b in range(BLOCKS)]
+        spin = [banks.tile([Q, BANK], F32, name=f"spin{k}", tag="bank") for k in range(len(PIECES))]
+        squared = shared.tile([Q, N], F32, name="squared", tag="squared_then_hidden")
+        gau = held.tile([Q, N], F32, name="gau")
         for b in range(BLOCKS):
-            for k in range(PIECES):
-                product = held.tile([P, PIECE], F32, name=f"product{b}_{k}")
+            for k, cols in enumerate(PIECES):
+                width = WIDTHS[k]
+                listed = slice(STARTS[k] // 16, (STARTS[k] + width) // 16)
                 nc.vector.tensor_tensor(
-                    product[:],
-                    table[b][:].indirect(offsets[:, k * OFFSET_COLS : (k + 1) * OFFSET_COLS]),
-                    target[b][k][:],
+                    product[b][:, cols],
+                    table[b][:].indirect(offsets[:, listed]),
+                    target[b][:, cols],
                     MULT,
                 )
-                nc.tensor.matmul(spin[k][:], ones[:], product[:], start=(b == 0), stop=(b == BLOCKS - 1))
+                nc.tensor.matmul(
+                    spin[k][:, :width], ones[:], product[b][:, cols], start=(b == 0), stop=(b == BLOCKS - 1)
+                )
                 if b == BLOCKS - 1:
-                    squared = held.tile([Q, PIECE], F32, name=f"squared{k}")
-                    nc.scalar.activation(squared[:], spin[k][:], FUNC.Square, bias=minus_centers[:])
-                    nc.scalar.activation(gau[k][:], squared[:], FUNC.Exp, scale=-8.0)
-                    nc.gpsimd.tensor_copy(gau_bf[k][:], gau[k][:])
+                    nc.scalar.activation(squared[:, cols], spin[k][:, :width], FUNC.Square, bias=minus_centers[:])
+                    nc.scalar.activation(gau[:, cols], squared[:, cols], FUNC.Exp, scale=-8.0)
 
-        hidden = []
-        for k in range(PIECES):
-            z1 = banks.tile([Q, PIECE], F32, name=f"z1_{k}", tag="bank")
-            nc.tensor.matmul(z1[:], w1_sb[:], gau_bf[k][:], start=True, stop=True)
-            hidden.append(held.tile([Q, PIECE], BF16, name=f"hidden{k}"))
-            nc.scalar.activation(hidden[k][:], z1[:], FUNC.Silu, bias=b1_sb[:])
-        for k in range(PIECES):
-            z2 = banks.tile([Q, PIECE], F32, name=f"z2_{k}", tag="bank")
-            nc.tensor.matmul(z2[:], w2_sb[:], hidden[k][:], start=True, stop=True)
-            layer = held.tile([Q, PIECE], F32, name=f"layer{k}")
-            nc.scalar.activation(layer[:], z2[:], FUNC.Silu, bias=b2_sb[:])
-            result = held.tile([Q, PIECE], F32, name=f"result{k}")
-            nc.vector.tensor_tensor(result[:], layer[:], gau[k][:], ADD)
-            nc.sync.dma_start(out[:, k * PIECE : (k + 1) * PIECE], result[:])
+        gau_bf = held.tile([Q, N], BF16, name="gau_bf")
+        for cols in PIECES:
+            nc.vector.tensor_copy(gau_bf[:, cols], gau[:, cols])
+
+        hidden = shared.tile([Q, N], BF16, name="hidden", tag="squared_then_hidden")
+        for k, cols in enumerate(PIECES):
+            width = WIDTHS[k]
+            z1 = banks.tile([Q, BANK], F32, name=f"z1_{k}", tag="bank")
+            nc.tensor.matmul(z1[:, :width], w1_sb[:], gau_bf[:, cols], start=True, stop=True)
+            nc.scalar.activation(hidden[:, cols], z1[:, :width], FUNC.Silu, bias=b1_sb[:])
+        layer = held.tile([Q, N], F32, name="layer")
+        result = held.tile([Q, N], F32, name="result")
+        for k, cols in enumerate(PIECES):
+            width = WIDTHS[k]
+            z2 = banks.tile([Q, BANK], F32, name=f"z2_{k}", tag="bank")
+            nc.tensor.matmul(z2[:, :width], w2_sb[:], hidden[:, cols], start=True, stop=True)
+            nc.scalar.activation(layer[:, cols], z2[:, :width], FUNC.Silu, bias=b2_sb[:])
+            nc.vector.tensor_tensor(result[:, cols], layer[:, cols], gau[:, cols], ADD)
+            nc.sync.dma_start(out[:, cols], result[:, cols])

@@ -11,7 +11,7 @@ P = 128
 C, S, N, Q = 256, 4096, 2048, 128
 BLOCKS = C // P
 BANK = 512
-WIDTHS = (512, 512, 512, 256, 256)
+WIDTHS = (128, 384, 512, 512, 256, 256)
 assert sum(WIDTHS) == N and max(WIDTHS) <= BANK
 STARTS = [sum(WIDTHS[:k]) for k in range(len(WIDTHS))]
 PIECES = [slice(start, start + width) for start, width in zip(STARTS, WIDTHS)]
@@ -28,6 +28,8 @@ def tile_spindistanceedge_kernel(tc, x, other, centers, w1, b1, w2, b2, offs, ou
     ):
         offsets = held.tile([P, N // 16], U16, name="offsets")
         nc.sync.dma_start(offsets[:], offs)
+        centers_sb = held.tile([Q, 1], F32, name="centers_sb")
+        nc.sync.dma_start(centers_sb[:], centers)
         table = []
         target = []
         for b in range(BLOCKS):
@@ -37,14 +39,12 @@ def tile_spindistanceedge_kernel(tc, x, other, centers, w1, b1, w2, b2, offs, ou
             target.append(held.tile([P, N], F32, name=f"target{b}"))
             for start in range(0, N, BANK):
                 nc.sync.dma_start(target[b][:, start : start + BANK], other[rows, start : start + BANK])
-
         w1_sb = held.tile([Q, Q], BF16, name="w1_sb")
         w2_sb = held.tile([Q, Q], BF16, name="w2_sb")
-        centers_sb = held.tile([Q, 1], F32, name="centers_sb")
         b1_sb = held.tile([Q, 1], F32, name="b1_sb")
         b2_sb = held.tile([Q, 1], F32, name="b2_sb")
-        for tile, source in ((centers_sb, centers), (w1_sb, w1), (b1_sb, b1), (w2_sb, w2), (b2_sb, b2)):
-            nc.scalar.dma_start(tile[:], source)
+        for tile, source in ((w1_sb, w1), (b1_sb, b1), (w2_sb, w2), (b2_sb, b2)):
+            nc.sync.dma_start(tile[:], source)
 
         ones = held.tile([P, Q], F32, name="ones")
         nc.gpsimd.memset(ones[:], 1.0)

@@ -11,7 +11,7 @@ P = 128
 C, S, N, Q = 256, 4096, 2048, 128
 BLOCKS = C // P
 BANK = 512
-WIDTHS = (128, 384, 512, 512, 256, 256)
+WIDTHS = (256,) * 8
 assert sum(WIDTHS) == N and max(WIDTHS) <= BANK
 STARTS = [sum(WIDTHS[:k]) for k in range(len(WIDTHS))]
 PIECES = [slice(start, start + width) for start, width in zip(STARTS, WIDTHS)]

@@ -15,6 +15,7 @@ WIDTHS = (256,) * 8
 assert sum(WIDTHS) == N and max(WIDTHS) <= BANK
 STARTS = [sum(WIDTHS[:k]) for k in range(len(WIDTHS))]
 PIECES = [slice(start, start + width) for start, width in zip(STARTS, WIDTHS)]
+LAG = 4
 
 FLOPS = 2 * C * N + 2 * (2 * Q * Q * N)
 
@@ -77,17 +78,18 @@ def tile_spindistanceedge_kernel(tc, x, other, centers, w1, b1, w2, b2, offs, ou
             nc.vector.tensor_copy(gau_bf[:, cols], gau[:, cols])
 
         hidden = shared.tile([Q, N], BF16, name="hidden", tag="squared_then_hidden")
-        for k, cols in enumerate(PIECES):
-            width = WIDTHS[k]
-            z1 = banks.tile([Q, BANK], F32, name=f"z1_{k}", tag="bank")
-            nc.tensor.matmul(z1[:, :width], w1_sb[:], gau_bf[:, cols], start=True, stop=True)
-            nc.scalar.activation(hidden[:, cols], z1[:, :width], FUNC.Silu, bias=b1_sb[:])
         layer = held.tile([Q, N], F32, name="layer")
         result = held.tile([Q, N], F32, name="result")
-        for k, cols in enumerate(PIECES):
-            width = WIDTHS[k]
-            z2 = banks.tile([Q, BANK], F32, name=f"z2_{k}", tag="bank")
-            nc.tensor.matmul(z2[:, :width], w2_sb[:], hidden[:, cols], start=True, stop=True)
-            nc.scalar.activation(layer[:, cols], z2[:, :width], FUNC.Silu, bias=b2_sb[:])
-            nc.vector.tensor_tensor(result[:, cols], layer[:, cols], gau[:, cols], ADD)
-            nc.sync.dma_start(out[:, cols], result[:, cols])
+        for step in range(len(PIECES) + LAG):
+            if step < len(PIECES):
+                cols, width = PIECES[step], WIDTHS[step]
+                z1 = banks.tile([Q, BANK], F32, name=f"z1_{step}", tag="bank")
+                nc.tensor.matmul(z1[:, :width], w1_sb[:], gau_bf[:, cols], start=True, stop=True)
+                nc.scalar.activation(hidden[:, cols], z1[:, :width], FUNC.Silu, bias=b1_sb[:])
+            if step >= LAG:
+                cols, width = PIECES[step - LAG], WIDTHS[step - LAG]
+                z2 = banks.tile([Q, BANK], F32, name=f"z2_{step - LAG}", tag="bank")
+                nc.tensor.matmul(z2[:, :width], w2_sb[:], hidden[:, cols], start=True, stop=True)
+                nc.scalar.activation(layer[:, cols], z2[:, :width], FUNC.Silu, bias=b2_sb[:])
+                nc.vector.tensor_tensor(result[:, cols], layer[:, cols], gau[:, cols], ADD)
+                nc.sync.dma_start(out[:, cols], result[:, cols])

@@ -11,7 +11,7 @@ P = 128
 C, S, N, Q = 256, 4096, 2048, 128
 BLOCKS = C // P
 BANK = 512
-WIDTHS = (256,) * 8
+WIDTHS = (320, 288, 288, 256, 256, 224, 224, 192)
 assert sum(WIDTHS) == N and max(WIDTHS) <= BANK
 STARTS = [sum(WIDTHS[:k]) for k in range(len(WIDTHS))]
 PIECES = [slice(start, start + width) for start, width in zip(STARTS, WIDTHS)]

@@ -15,7 +15,8 @@ WIDTHS = (320, 288, 288, 256, 256, 224, 224, 192)
 assert sum(WIDTHS) == N and max(WIDTHS) <= BANK
 STARTS = [sum(WIDTHS[:k]) for k in range(len(WIDTHS))]
 PIECES = [slice(start, start + width) for start, width in zip(STARTS, WIDTHS)]
-LAG = 4
+HALF = BANK // 2
+LAG = 2
 
 FLOPS = 2 * C * N + 2 * (2 * Q * Q * N)
 
@@ -80,16 +81,18 @@ def tile_spindistanceedge_kernel(tc, x, other, centers, w1, b1, w2, b2, offs, ou
         hidden = shared.tile([Q, N], BF16, name="hidden", tag="squared_then_hidden")
         layer = held.tile([Q, N], F32, name="layer")
         result = held.tile([Q, N], F32, name="result")
-        for step in range(len(PIECES) + LAG):
-            if step < len(PIECES):
-                cols, width = PIECES[step], WIDTHS[step]
+        chunks = N // BANK
+        for step in range(chunks + LAG):
+            if step < chunks:
+                cols = slice(step * BANK, (step + 1) * BANK)
                 z1 = banks.tile([Q, BANK], F32, name=f"z1_{step}", tag="bank")
-                nc.tensor.matmul(z1[:, :width], w1_sb[:], gau_bf[:, cols], start=True, stop=True)
-                nc.scalar.activation(hidden[:, cols], z1[:, :width], FUNC.Silu, bias=b1_sb[:])
+                nc.tensor.matmul(z1[:], w1_sb[:], gau_bf[:, cols], start=True, stop=True)
+                nc.scalar.activation(hidden[:, cols], z1[:], FUNC.Silu, bias=b1_sb[:])
             if step >= LAG:
-                cols, width = PIECES[step - LAG], WIDTHS[step - LAG]
-                z2 = banks.tile([Q, BANK], F32, name=f"z2_{step - LAG}", tag="bank")
-                nc.tensor.matmul(z2[:, :width], w2_sb[:], hidden[:, cols], start=True, stop=True)
-                nc.scalar.activation(layer[:, cols], z2[:, :width], FUNC.Silu, bias=b2_sb[:])
-                nc.vector.tensor_tensor(result[:, cols], layer[:, cols], gau[:, cols], ADD)
-                nc.sync.dma_start(out[:, cols], result[:, cols])
+                for start in ((step - LAG) * BANK, (step - LAG) * BANK + HALF):
+                    cols = slice(start, start + HALF)
+                    z2 = banks.tile([Q, BANK], F32, name=f"z2_{start}", tag="bank")
+                    nc.tensor.matmul(z2[:, :HALF], w2_sb[:], hidden[:, cols], start=True, stop=True)
+                    nc.scalar.activation(layer[:, cols], z2[:, :HALF], FUNC.Silu, bias=b2_sb[:])
+                    nc.vector.tensor_tensor(result[:, cols], layer[:, cols], gau[:, cols], ADD)
+                    nc.sync.dma_start(out[:, cols], result[:, cols])

@@ -15,6 +15,10 @@ WIDTHS = (320, 288, 288, 256, 256, 224, 224, 192)
 assert sum(WIDTHS) == N and max(WIDTHS) <= BANK
 STARTS = [sum(WIDTHS[:k]) for k in range(len(WIDTHS))]
 PIECES = [slice(start, start + width) for start, width in zip(STARTS, WIDTHS)]
+PARTS = (
+    [(start, start + BANK) for start in range(0, N, BANK)],
+    [(0, STARTS[1]), (STARTS[1], STARTS[3]), (STARTS[3], STARTS[5]), (STARTS[5], N)],
+)
 HALF = BANK // 2
 LAG = 2
 
@@ -39,8 +43,8 @@ def tile_spindistanceedge_kernel(tc, x, other, centers, w1, b1, w2, b2, offs, ou
             table.append(held.tile([P, S], F32, name=f"table{b}"))
             nc.sync.dma_start(table[b][:], x[rows, :])
             target.append(held.tile([P, N], F32, name=f"target{b}"))
-            for start in range(0, N, BANK):
-                nc.sync.dma_start(target[b][:, start : start + BANK], other[rows, start : start + BANK])
+            for start, stop in PARTS[b]:
+                nc.sync.dma_start(target[b][:, start:stop], other[rows, start:stop])
         w1_sb = held.tile([Q, Q], BF16, name="w1_sb")
         w2_sb = held.tile([Q, Q], BF16, name="w2_sb")
         b1_sb = held.tile([Q, 1], F32, name="b1_sb")

import concourse.mybir as mybir

F32 = mybir.dt.float32
BF16 = mybir.dt.bfloat16
U16 = mybir.dt.uint16
FUNC = mybir.ActivationFunctionType
MULT = mybir.AluOpType.mult
ADD = mybir.AluOpType.add

P = 128
C, S, N, Q = 256, 4096, 2048, 128
BLOCKS = C // P
BANK = 512
WIDTHS = (320, 288, 288, 256, 256, 224, 224, 192)
assert sum(WIDTHS) == N and max(WIDTHS) <= BANK
STARTS = [sum(WIDTHS[:k]) for k in range(len(WIDTHS))]
PIECES = [slice(start, start + width) for start, width in zip(STARTS, WIDTHS)]
PARTS = (
    [(start, start + BANK) for start in range(0, N, BANK)],
    [(0, STARTS[1]), (STARTS[1], STARTS[3]), (STARTS[3], STARTS[5]), (STARTS[5], N)],
)
HALF = BANK // 2
LAG = 2

FLOPS = 2 * C * N + 2 * (2 * Q * Q * N)


def tile_spindistanceedge_kernel(tc, x, other, centers, w1, b1, w2, b2, offs, out):
    nc = tc.nc
    with (
        tc.tile_pool(name="held", bufs=1) as held,
        tc.tile_pool(name="shared", bufs=1) as shared,
        tc.psum_pool(name="banks", bufs=8) as banks,
    ):
        offsets = held.tile([P, N // 16], U16, name="offsets")
        nc.sync.dma_start(offsets[:], offs)
        centers_sb = held.tile([Q, 1], F32, name="centers_sb")
        nc.sync.dma_start(centers_sb[:], centers)
        table = []
        target = []
        for b in range(BLOCKS):
            rows = slice(b * P, (b + 1) * P)
            table.append(held.tile([P, S], F32, name=f"table{b}"))
            nc.sync.dma_start(table[b][:], x[rows, :])
            target.append(held.tile([P, N], F32, name=f"target{b}"))
            for start, stop in PARTS[b]:
                nc.sync.dma_start(target[b][:, start:stop], other[rows, start:stop])
        w1_sb = held.tile([Q, Q], BF16, name="w1_sb")
        w2_sb = held.tile([Q, Q], BF16, name="w2_sb")
        b1_sb = held.tile([Q, 1], F32, name="b1_sb")
        b2_sb = held.tile([Q, 1], F32, name="b2_sb")
        for tile, source in ((w1_sb, w1), (b1_sb, b1), (w2_sb, w2), (b2_sb, b2)):
            nc.sync.dma_start(tile[:], source)

        ones = held.tile([P, Q], F32, name="ones")
        nc.gpsimd.memset(ones[:], 1.0)
        minus_centers = held.tile([Q, 1], F32, name="minus_centers")
        nc.scalar.mul(minus_centers[:], centers_sb[:], -1.0)

        product = [held.tile([P, N], F32, name=f"product{b}") for b in range(BLOCKS)]
        spin = [banks.tile([Q, BANK], F32, name=f"spin{k}", tag="bank") for k in range(len(PIECES))]
        squared = shared.tile([Q, N], F32, name="squared", tag="squared_then_hidden")
        gau = held.tile([Q, N], F32, name="gau")
        for b in range(BLOCKS):
            for k, cols in enumerate(PIECES):
                width = WIDTHS[k]
                listed = slice(STARTS[k] // 16, (STARTS[k] + width) // 16)
                nc.vector.tensor_tensor(
                    product[b][:, cols],
                    table[b][:].indirect(offsets[:, listed]),
                    target[b][:, cols],
                    MULT,
                )
                nc.tensor.matmul(
                    spin[k][:, :width], ones[:], product[b][:, cols], start=(b == 0), stop=(b == BLOCKS - 1)
                )
                if b == BLOCKS - 1:
                    nc.scalar.activation(squared[:, cols], spin[k][:, :width], FUNC.Square, bias=minus_centers[:])
                    nc.scalar.activation(gau[:, cols], squared[:, cols], FUNC.Exp, scale=-8.0)

        gau_bf = held.tile([Q, N], BF16, name="gau_bf")
        for cols in PIECES:
            nc.vector.tensor_copy(gau_bf[:, cols], gau[:, cols])

        hidden = shared.tile([Q, N], BF16, name="hidden", tag="squared_then_hidden")
        layer = held.tile([Q, N], F32, name="layer")
        result = held.tile([Q, N], F32, name="result")
        chunks = N // BANK
        for step in range(chunks + LAG):
            if step < chunks:
                cols = slice(step * BANK, (step + 1) * BANK)
                z1 = banks.tile([Q, BANK], F32, name=f"z1_{step}", tag="bank")
                nc.tensor.matmul(z1[:], w1_sb[:], gau_bf[:, cols], start=True, stop=True)
                nc.scalar.activation(hidden[:, cols], z1[:], FUNC.Silu, bias=b1_sb[:])
            if step >= LAG:
                for start in ((step - LAG) * BANK, (step - LAG) * BANK + HALF):
                    cols = slice(start, start + HALF)
                    z2 = banks.tile([Q, BANK], F32, name=f"z2_{start}", tag="bank")
                    nc.tensor.matmul(z2[:, :HALF], w2_sb[:], hidden[:, cols], start=True, stop=True)
                    nc.scalar.activation(layer[:, cols], z2[:, :HALF], FUNC.Silu, bias=b2_sb[:])
                    nc.vector.tensor_tensor(result[:, cols], layer[:, cols], gau[:, cols], ADD)
                    nc.sync.dma_start(out[:, cols], result[:, cols])
